import numpy as np
import ml_dtypes


def mxq(x, axis, fmt="e4m3"):
    dtype, down = {"e4m3": (ml_dtypes.float8_e4m3fn, 7), "e5m2": (ml_dtypes.float8_e5m2, 14)}[fmt]
    v = np.moveaxis(np.asarray(x, np.float32).astype(ml_dtypes.bfloat16).astype(np.float64), axis, -1)
    blocks = v.reshape(v.shape[:-1] + (-1, 32))
    amax = np.abs(blocks).max(-1, keepdims=True)
    byte = np.maximum(np.where(amax > 0, np.frexp(amax)[1] - 1 + 127, 0) - down, 1)
    scale = np.exp2(byte - 127.0)
    codes = (blocks / scale).astype(np.float32).astype(dtype).astype(np.float64)
    return np.moveaxis((codes * scale).reshape(v.shape), -1, axis)


WIDE = False


def mx_kscale(k):
    if not WIDE:
        return np.ones(k)
    levels = np.array([10, -10, 5, -5, 0])
    if k % 512:
        return np.exp2(np.random.permutation(np.resize(levels, k // 32))).repeat(32)
    a = np.empty((k // 512, 16))
    for p in range(k // 512):
        a[p, :8] = np.random.permutation(np.resize(levels, 8))
        for g in range(8):
            far = levels[np.abs(levels - a[p, g]) >= 10]
            a[p, g + 8] = far[np.random.randint(len(far))]
    return np.exp2(a.ravel()).repeat(32)


BF16 = ml_dtypes.bfloat16


def bf(x):
    return np.asarray(x, np.float32).astype(BF16)


def f64(x):
    return np.asarray(x).astype(np.float64)


B, S, DIM, H, NOPE, ROPE_D, VD = 4, 1024, 1024, 2, 64, 64, 128
QKD = NOPE + ROPE_D
BASE = 10000.0


def rope_cos_sin(seq_len):
    theta = 1.0 / BASE ** (f64(np.arange(0, ROPE_D, 2)) / ROPE_D)
    pos = f64(np.arange(seq_len))
    ang = pos[:, None] * theta[None, :]
    return np.cos(ang), np.sin(ang)


def apply_rope(v, cos, sin):
    b, s, h, d = v.shape
    vs = v.reshape(b, s, h, d // 2, 2)
    c = cos[None, :, None, :]
    sn = sin[None, :, None, :]
    out = np.stack([vs[..., 0] * c - vs[..., 1] * sn, vs[..., 1] * c + vs[..., 0] * sn], axis=-1)
    return out.reshape(b, s, h, d)


def setup_inputs():
    s = mx_kscale(DIM)
    return {'x': bf(np.random.standard_normal((B, S, DIM)) * s),
            'Wq': bf(np.random.standard_normal((DIM, H * QKD)) / np.sqrt(DIM) / s[:, None]),
            'Wk': bf(np.random.standard_normal((DIM, H * QKD)) / np.sqrt(DIM) / s[:, None])}


def reference(x, Wq, Wk):
    xq = mxq(f64(x), 2, 'e4m3')
    q = (xq @ mxq(f64(Wq), 0, 'e4m3')).reshape(B, S, H, QKD)
    k = (xq @ mxq(f64(Wk), 0, 'e4m3')).reshape(B, S, H, QKD)
    cos, sin = rope_cos_sin(S)
    q = np.concatenate([q[..., :NOPE], apply_rope(q[..., NOPE:], cos, sin)], axis=-1)
    k = np.concatenate([k[..., :NOPE], apply_rope(k[..., NOPE:], cos, sin)], axis=-1)
    return q, k

@@ -1,0 +1,264 @@
+import math
+from contextlib import ExitStack
+
+import concourse.mybir as mybir
+from concourse.masks import make_identity
+
+F32 = mybir.dt.float32
+BF16 = mybir.dt.bfloat16
+I32 = mybir.dt.int32
+U32 = mybir.dt.uint32
+U8 = mybir.dt.uint8
+FP8X4 = mybir.dt.float8_e4m3fn_x4
+ALU = mybir.AluOpType
+ACT = mybir.ActivationFunctionType
+
+P = 128
+B = 4
+T = 8
+DIM = 1024
+NPAIRS = 32
+RATIO = 10000.0 ** (-1.0 / 32.0)
+ROPE = 0
+NOPE = 1
+FLOPS = 2 * 4096 * 1024 * 512
+
+N_UNITS = 16
+GP_ADD_UNTIL = 15
+S_REGROUP = ((1, 1, 0), (1, 1, 1))
+
+
+def tile_mla_pa_t_kernel(tc, x, Wq, Wk, out_0, out_1):
+    nc = tc.nc
+    with ExitStack() as ctx:
+        ctx.enter_context(tc.manual_schedule())
+        keep = ctx.enter_context(tc.tile_pool(name="keep", bufs=1))
+        work = ctx.enter_context(tc.tile_pool(name="work", bufs=4))
+        ps_t = ctx.enter_context(tc.psum_pool(name="ps_t", bufs=4))
+        ps_r = ctx.enter_context(tc.psum_pool(name="ps_r", bufs=2))
+        ps_n = ctx.enter_context(tc.psum_pool(name="ps_n", bufs=2))
+
+        x_view = x.rearrange("b (p t) k -> b p t k", t=T)
+        out_views = [o.rearrange("b (p t) h d -> b p t (h d)", t=T) for o in (out_0, out_1)]
+
+        chunks = [(0, 0, 1), (0, 1, 1), (0, 2, 2), (0, 4, 2), (0, 6, 2), (1, 0, 4), (1, 4, 4), (2, 0, 8), (3, 0, 8)]
+        x_words = {}
+        wraw = keep.tile([P, 2, 8, 256], BF16, name="wraw")
+        for g in range(2):
+            for qk, w_dram in enumerate((Wq, Wk)):
+                nc.sync.dma_start(
+                    out=wraw[:, qk, 4 * g : 4 * g + 4, :],
+                    in_=w_dram.rearrange("(g p t) c -> g p t c", g=2, t=4)[g],
+                )
+        for b, t0, nt in chunks:
+            xs = keep.tile([P, nt, DIM], BF16, name="x%d_%d" % (b, t0))
+            nc.sync.dma_start(out=xs[:], in_=x_view[b][:, t0 : t0 + nt, :])
+            for t in range(nt):
+                x_words[(b, t0 + t)] = xs[:, t, :].bitcast(F32)
+
+        zero = keep.tile([P, 1], F32, name="zero")
+        nc.vector.memset(zero[:], 0.0)
+        warm = keep.tile([P, 1], F32, name="warm")
+        nc.scalar.activation(out=warm[:], in_=zero[:], func=ACT.Sin)
+        pos_i = keep.tile([P, T], I32, name="pos_i")
+        nc.gpsimd.iota(pos_i[:], pattern=[[1, T]], base=0, channel_multiplier=T)
+        ident = keep.tile([P, P], F32, name="ident")
+        make_identity(nc, ident[:])
+
+        turns = keep.tile([P, T, NPAIRS], F32, name="turns")
+        nc.vector.tensor_scalar(
+            out=turns[:, :, 0:1], in0=pos_i[:].unsqueeze(2), scalar1=1.0 / (2.0 * math.pi), scalar2=None, op0=ALU.mult
+        )
+        for level in range(5):
+            w = 1 << level
+            nc.vector.tensor_scalar(
+                out=turns[:, :, w : 2 * w], in0=turns[:, :, 0:w], scalar1=RATIO**w, scalar2=None, op0=ALU.mult
+            )
+        whole = keep.tile([P, 2, T, NPAIRS], I32, name="whole")
+        nc.vector.tensor_scalar(out=whole[:, 0], in0=turns[:], scalar1=0.25, scalar2=None, op0=ALU.add)
+        nc.vector.tensor_copy(out=whole[:, 1], in_=turns[:])
+        frac = keep.tile([P, 2, T, NPAIRS], F32, name="frac")
+        nc.vector.tensor_tensor(out=frac[:, 0], in0=whole[:, 0], in1=turns[:], op=ALU.subtract)
+        nc.vector.scalar_tensor_tensor(
+            out=frac[:, 1], in0=whole[:, 1], scalar=0.25, in1=turns[:], op0=ALU.add, op1=ALU.subtract
+        )
+        half_sin = keep.tile([P, 2, T, NPAIRS], F32, name="half_sin")
+        nc.scalar.activation(out=half_sin[:], in_=frac[:], func=ACT.Sin, scale=math.pi)
+        half_sq = keep.tile([P, 2, T, NPAIRS], F32, name="half_sq")
+        nc.scalar.activation(out=half_sq[:], in_=half_sin[:], func=ACT.Square)
+        cos_t = keep.tile([P, T, 2, 2 * NPAIRS], F32, name="cos_t")
+        sin_t = keep.tile([P, T, 2, NPAIRS, 2], F32, name="sin_t")
+
+        def tables():
+            for h in range(2):
+                nc.vector.tensor_scalar(
+                    out=cos_t[:, :, h, :].rearrange("p t (i e) -> p t i e", e=2),
+                    in0=half_sq[:, 0].unsqueeze(3).to_broadcast([P, T, NPAIRS, 2]),
+                    scalar1=-2.0,
+                    scalar2=1.0,
+                    op0=ALU.mult,
+                    op1=ALU.add,
+                )
+            for e, sign in ((0, -1.0), (1, 1.0)):
+                nc.vector.tensor_scalar(
+                    out=sin_t[:, :, :, :, e],
+                    in0=half_sq[:, 1].unsqueeze(2).to_broadcast([P, T, 2, NPAIRS]),
+                    scalar1=-2.0 * sign,
+                    scalar2=sign,
+                    op0=ALU.mult,
+                    op1=ALU.add,
+                )
+
+        wgrp = keep.tile([P, 2, 2, 2, 2, 64, 4], BF16, name="wgrp", align_bytes=64)
+        wcodes = keep.tile([P, 2, 512], U32, name="wcodes", align_bytes=64)
+        wscales = keep.tile([P, 2, 512], U8, name="wscales", align_bytes=64)
+        for g in range(2):
+            for s in (ROPE, NOPE):
+                for qk in range(2):
+                    src = wraw[:, qk, 4 * g : 4 * g + 4, :].rearrange("p t (h s c) -> p t h s c", h=2, s=2)
+                    permuted = src[:, :, :, 1 - s, :].rearrange("p t h c -> p h c t")
+                    if (g, s, qk) in S_REGROUP:
+                        nc.scalar.copy(out=wgrp[:, g, s, qk], in_=permuted)
+                    else:
+                        nc.vector.tensor_copy(out=wgrp[:, g, s, qk], in_=permuted)
+            nc.vector.quantize_mx(
+                out=wcodes[:, g, :].bitcast(FP8X4),
+                scales=wscales[:, g, :],
+                in_=wgrp[:, g].rearrange("p s q h c t -> p (s q h c t)"),
+            )
+
+        groups = [(n, n + 1) for n in range(0, N_UNITS - 2, 2)] + [(N_UNITS - 2,), (N_UNITS - 1,)]
+        out_of = {}
+        last_of = {}
+        for group in groups:
+            og = keep.tile([P, len(group), 2, 512], F32, name="og%d" % group[0])
+            for u, n in enumerate(group):
+                out_of[n] = og[:, u]
+            last_of[group[-1]] = (og, group)
+        live = {}
+
+        def where(n):
+            return n // 4, 2 * (n % 4)
+
+        def transposes(n):
+            b, t0 = where(n)
+            for a in range(2):
+                xt = ps_t.tile([P, 4, P], F32, name="xt")
+                for j in range(4):
+                    nc.tensor.transpose(
+                        out=xt[:, j, :], in_=x_words[(b, t0 + a)][:, 256 * (j // 2) + j % 2 : 256 * (j // 2 + 1) : 2], identity=ident[:]
+                    )
+                live[("xt", n, a)] = xt
+
+        def regroup(n):
+            grp = work.tile([P, 2, 2, P, 4], BF16, name="grp", align_bytes=64)
+            grp_words = grp[:].bitcast(F32)
+            for a in range(2):
+                nc.scalar.copy(
+                    out=grp_words[:, a], in_=live[("xt", n, a)][:].rearrange("p (g u) r -> p g r u", u=2)
+                )
+            live[("grp", n)] = grp
+
+        def quantise(n, pieces):
+            grp = live[("grp", n)][:].rearrange("p a g r t -> p (a g r t)")
+            codes = work.tile([P, 512], U32, name="codes", align_bytes=64)
+            scales = work.tile([P, 512], U8, name="scales", align_bytes=64)
+            width = 512 // pieces
+            for piece in range(pieces):
+                cols = slice(piece * width, (piece + 1) * width)
+                nc.vector.quantize_mx(
+                    out=codes[:, cols].bitcast(FP8X4),
+                    scales=scales[:, cols],
+                    in_=grp[:, 4 * piece * width : 4 * (piece + 1) * width],
+                )
+            live[("q", n)] = (codes, scales)
+
+        def multiply(n):
+            codes, scales = live[("q", n)]
+            rope = ps_r.tile([P, 512], F32, name="rope")
+            nope = ps_n.tile([P, 512], F32, name="nope")
+            for s, bank in ((ROPE, rope), (NOPE, nope)):
+                for a in range(2):
+                    for g in range(2):
+                        col = (2 * a + g) * P
+                        nc.tensor.matmul_mx(
+                            out=bank[:, 256 * a : 256 * a + 256],
+                            lhsT=codes[:, col : col + P].bitcast(FP8X4),
+                            lhsT_scale=scales[:, col : col + P],
+                            rhs=wcodes[:, g, 256 * s : 256 * s + 256].bitcast(FP8X4),
+                            rhs_scale=wscales[:, g, 256 * s : 256 * s + 256],
+                            start=(g == 0),
+                            stop=(g == 1),
+                        )
+            live[("rope", n)] = rope
+            live[("nope", n)] = nope
+
+        def plain_out(n):
+            b, t0 = where(n)
+            dst = out_of[n].rearrange("p q (a h s c) -> p q a h s c", a=2, h=2, s=2)
+            nc.scalar.copy(
+                out=dst[:, :, :, :, 0, :],
+                in_=live[("nope", n)][:].rearrange("p (a q h c) -> p q a h c", a=2, q=2, h=2),
+            )
+
+        def products(n):
+            b, t0 = where(n)
+            rope = live[("rope", n)]
+            dst = out_of[n].rearrange("p q (a h s c) -> p q a h s c", a=2, h=2, s=2)
+            nc.vector.tensor_tensor(
+                out=dst[:, :, :, :, 1, :],
+                in0=rope[:].rearrange("p (a q h c) -> p q a h c", a=2, q=2, h=2),
+                in1=cos_t[:, t0 : t0 + 2].unsqueeze(1).to_broadcast([P, 2, 2, 2, 2 * NPAIRS]),
+                op=ALU.mult,
+            )
+            cross = work.tile([P, 2, 2, 2 * NPAIRS, 2], F32, name="cross")
+            nc.vector.tensor_tensor(
+                out=cross[:],
+                in0=rope[:].rearrange("p (a q hi e) -> p a q hi e", a=2, q=2, e=2)[:, :, :, :, ::-1],
+                in1=sin_t[:, t0 : t0 + 2]
+                .rearrange("p a h i e -> p a (h i) e")
+                .unsqueeze(2)
+                .to_broadcast([P, 2, 2, 2 * NPAIRS, 2]),
+                op=ALU.mult,
+            )
+            live[("cross", n)] = cross
+
+        def add_and_store(n):
+            b, t0 = where(n)
+            eng = nc.gpsimd if n < GP_ADD_UNTIL else nc.vector
+            rot = out_of[n].rearrange("p q (a h s c) -> p q a h s c", a=2, h=2, s=2)
+            eng.tensor_tensor(
+                out=rot[:, :, :, :, 1, :],
+                in0=rot[:, :, :, :, 1, :],
+                in1=live[("cross", n)][:].rearrange("p a q (h i) e -> p q a h (i e)", h=2),
+                op=ALU.add,
+            )
+            if n in last_of:
+                og, group = last_of[n]
+                gb, gt0 = where(group[0])
+                for qk in range(2):
+                    nc.sync.dma_start(
+                        out=out_views[qk][gb][:, gt0 : gt0 + 2 * len(group), :].rearrange("p (u a) d -> p u (a d)", a=2),
+                        in_=og[:, :, qk, :],
+                    )
+
+        def prepare(n, pieces):
+            transposes(n)
+            regroup(n)
+            quantise(n, pieces)
+
+        def finish(n):
+            multiply(n)
+            products(n)
+            plain_out(n)
+            add_and_store(n)
+
+        prepare(0, 2)
+        prepare(1, 1)
+        tables()
+        finish(0)
+        prepare(2, 1)
+        for n in range(1, N_UNITS):
+            if n + 2 < N_UNITS:
+                prepare(n + 2, 1)
+            finish(n)

@@ -25,7 +25,9 @@ FLOPS = 2 * 4096 * 1024 * 512
 
 N_UNITS = 16
 GP_ADD_UNTIL = 15
-S_REGROUP = ((1, 1, 0), (1, 1, 1))
+S_REGROUP = ((0, 1, 1), (1, 1, 1))
+AHEAD = 4
+QUANT_AHEAD = 2
 
 
 def tile_mla_pa_t_kernel(tc, x, Wq, Wk, out_0, out_1):
@@ -33,7 +35,7 @@ def tile_mla_pa_t_kernel(tc, x, Wq, Wk, out_0, out_1):
     with ExitStack() as ctx:
         ctx.enter_context(tc.manual_schedule())
         keep = ctx.enter_context(tc.tile_pool(name="keep", bufs=1))
-        work = ctx.enter_context(tc.tile_pool(name="work", bufs=4))
+        work = ctx.enter_context(tc.tile_pool(name="work", bufs=6))
         ps_t = ctx.enter_context(tc.psum_pool(name="ps_t", bufs=4))
         ps_r = ctx.enter_context(tc.psum_pool(name="ps_r", bufs=2))
         ps_n = ctx.enter_context(tc.psum_pool(name="ps_n", bufs=2))
@@ -41,20 +43,28 @@ def tile_mla_pa_t_kernel(tc, x, Wq, Wk, out_0, out_1):
         x_view = x.rearrange("b (p t) k -> b p t k", t=T)
         out_views = [o.rearrange("b (p t) h d -> b p t (h d)", t=T) for o in (out_0, out_1)]
 
-        chunks = [(0, 0, 1), (0, 1, 1), (0, 2, 2), (0, 4, 2), (0, 6, 2), (1, 0, 4), (1, 4, 4), (2, 0, 8), (3, 0, 8)]
+        chunks = [(0, 0, 1), (0, 1, 1), (0, 2, 1), (0, 3, 1), (0, 4, 2), (0, 6, 2), (1, 0, 4), (1, 4, 4), (2, 0, 8), (3, 0, 8)]
         x_words = {}
         wraw = keep.tile([P, 2, 8, 256], BF16, name="wraw")
-        for g in range(2):
+
+        def load_w(g):
             for qk, w_dram in enumerate((Wq, Wk)):
                 nc.sync.dma_start(
                     out=wraw[:, qk, 4 * g : 4 * g + 4, :],
                     in_=w_dram.rearrange("(g p t) c -> g p t c", g=2, t=4)[g],
                 )
-        for b, t0, nt in chunks:
+
+        def load_x(b, t0, nt):
             xs = keep.tile([P, nt, DIM], BF16, name="x%d_%d" % (b, t0))
             nc.sync.dma_start(out=xs[:], in_=x_view[b][:, t0 : t0 + nt, :])
             for t in range(nt):
                 x_words[(b, t0 + t)] = xs[:, t, :].bitcast(F32)
+
+        for i, chunk in enumerate(chunks):
+            load_x(*chunk)
+            if i == 1:
+                load_w(0)
+                load_w(1)
 
         zero = keep.tile([P, 1], F32, name="zero")
         nc.vector.memset(zero[:], 0.0)
@@ -87,7 +97,7 @@ def tile_mla_pa_t_kernel(tc, x, Wq, Wk, out_0, out_1):
         half_sq = keep.tile([P, 2, T, NPAIRS], F32, name="half_sq")
         nc.scalar.activation(out=half_sq[:], in_=half_sin[:], func=ACT.Square)
         cos_t = keep.tile([P, T, 2, 2 * NPAIRS], F32, name="cos_t")
-        sin_t = keep.tile([P, T, 2, NPAIRS, 2], F32, name="sin_t")
+        sin_t = keep.tile([P, T, NPAIRS, 2], F32, name="sin_t")
 
         def tables():
             for h in range(2):
@@ -101,8 +111,8 @@ def tile_mla_pa_t_kernel(tc, x, Wq, Wk, out_0, out_1):
                 )
             for e, sign in ((0, -1.0), (1, 1.0)):
                 nc.vector.tensor_scalar(
-                    out=sin_t[:, :, :, :, e],
-                    in0=half_sq[:, 1].unsqueeze(2).to_broadcast([P, T, 2, NPAIRS]),
+                    out=sin_t[:, :, :, e],
+                    in0=half_sq[:, 1],
                     scalar1=-2.0 * sign,
                     scalar2=sign,
                     op0=ALU.mult,
@@ -112,7 +122,8 @@ def tile_mla_pa_t_kernel(tc, x, Wq, Wk, out_0, out_1):
         wgrp = keep.tile([P, 2, 2, 2, 2, 64, 4], BF16, name="wgrp", align_bytes=64)
         wcodes = keep.tile([P, 2, 512], U32, name="wcodes", align_bytes=64)
         wscales = keep.tile([P, 2, 512], U8, name="wscales", align_bytes=64)
-        for g in range(2):
+
+        def regroup_weights(g):
             for s in (ROPE, NOPE):
                 for qk in range(2):
                     src = wraw[:, qk, 4 * g : 4 * g + 4, :].rearrange("p t (h s c) -> p t h s c", h=2, s=2)
@@ -121,6 +132,8 @@ def tile_mla_pa_t_kernel(tc, x, Wq, Wk, out_0, out_1):
                         nc.scalar.copy(out=wgrp[:, g, s, qk], in_=permuted)
                     else:
                         nc.vector.tensor_copy(out=wgrp[:, g, s, qk], in_=permuted)
+
+        def quantise_weights(g):
             nc.vector.quantize_mx(
                 out=wcodes[:, g, :].bitcast(FP8X4),
                 scales=wscales[:, g, :],
@@ -211,14 +224,11 @@ def tile_mla_pa_t_kernel(tc, x, Wq, Wk, out_0, out_1):
                 in1=cos_t[:, t0 : t0 + 2].unsqueeze(1).to_broadcast([P, 2, 2, 2, 2 * NPAIRS]),
                 op=ALU.mult,
             )
-            cross = work.tile([P, 2, 2, 2 * NPAIRS, 2], F32, name="cross")
+            cross = work.tile([P, 2, 4, NPAIRS, 2], F32, name="cross")
             nc.vector.tensor_tensor(
                 out=cross[:],
-                in0=rope[:].rearrange("p (a q hi e) -> p a q hi e", a=2, q=2, e=2)[:, :, :, :, ::-1],
-                in1=sin_t[:, t0 : t0 + 2]
-                .rearrange("p a h i e -> p a (h i) e")
-                .unsqueeze(2)
-                .to_broadcast([P, 2, 2, 2 * NPAIRS, 2]),
+                in0=rope[:].rearrange("p (a qh i e) -> p a qh i e", a=2, qh=4, e=2)[:, :, :, :, ::-1],
+                in1=sin_t[:, t0 : t0 + 2].unsqueeze(2).to_broadcast([P, 2, 4, NPAIRS, 2]),
                 op=ALU.mult,
             )
             live[("cross", n)] = cross
@@ -230,7 +240,7 @@ def tile_mla_pa_t_kernel(tc, x, Wq, Wk, out_0, out_1):
             eng.tensor_tensor(
                 out=rot[:, :, :, :, 1, :],
                 in0=rot[:, :, :, :, 1, :],
-                in1=live[("cross", n)][:].rearrange("p a q (h i) e -> p q a h (i e)", h=2),
+                in1=live[("cross", n)][:].rearrange("p a (q h) i e -> p q a h (i e)", h=2),
                 op=ALU.add,
             )
             if n in last_of:
@@ -242,23 +252,26 @@ def tile_mla_pa_t_kernel(tc, x, Wq, Wk, out_0, out_1):
                         in_=og[:, :, qk, :],
                     )
 
-        def prepare(n, pieces):
+        for n in range(AHEAD):
             transposes(n)
             regroup(n)
-            quantise(n, pieces)
-
-        def finish(n):
+            if n == 0:
+                regroup_weights(0)
+                regroup_weights(1)
+                quantise_weights(0)
+                quantise_weights(1)
+        for n in range(QUANT_AHEAD):
+            quantise(n, 1)
+            if n == 0:
+                tables()
+        for n in range(N_UNITS):
             multiply(n)
+            if n + AHEAD < N_UNITS:
+                transposes(n + AHEAD)
             products(n)
+            if n + QUANT_AHEAD < N_UNITS:
+                quantise(n + QUANT_AHEAD, 1)
             plain_out(n)
+            if n + AHEAD < N_UNITS:
+                regroup(n + AHEAD)
             add_and_store(n)
-
-        prepare(0, 2)
-        prepare(1, 1)
-        tables()
-        finish(0)
-        prepare(2, 1)
-        for n in range(1, N_UNITS):
-            if n + 2 < N_UNITS:
-                prepare(n + 2, 1)
-            finish(n)

@@ -25,9 +25,6 @@ FLOPS = 2 * 4096 * 1024 * 512
 
 N_UNITS = 16
 GP_ADD_UNTIL = 15
-S_REGROUP = ((0, 1, 1), (1, 1, 1))
-AHEAD = 4
-QUANT_AHEAD = 2
 
 
 def tile_mla_pa_t_kernel(tc, x, Wq, Wk, out_0, out_1):
@@ -60,11 +57,12 @@ def tile_mla_pa_t_kernel(tc, x, Wq, Wk, out_0, out_1):
             for t in range(nt):
                 x_words[(b, t0 + t)] = xs[:, t, :].bitcast(F32)
 
-        for i, chunk in enumerate(chunks):
+        load_w(0)
+        load_x(*chunks[0])
+        load_x(*chunks[1])
+        load_w(1)
+        for chunk in chunks[2:]:
             load_x(*chunk)
-            if i == 1:
-                load_w(0)
-                load_w(1)
 
         zero = keep.tile([P, 1], F32, name="zero")
         nc.vector.memset(zero[:], 0.0)
@@ -75,49 +73,37 @@ def tile_mla_pa_t_kernel(tc, x, Wq, Wk, out_0, out_1):
         ident = keep.tile([P, P], F32, name="ident")
         make_identity(nc, ident[:])
 
-        turns = keep.tile([P, T, NPAIRS], F32, name="turns")
-        nc.vector.tensor_scalar(
-            out=turns[:, :, 0:1], in0=pos_i[:].unsqueeze(2), scalar1=1.0 / (2.0 * math.pi), scalar2=None, op0=ALU.mult
-        )
+        turns = keep.tile([P, T, NPAIRS, 2], F32, name="turns")
+        for e, sign in ((0, -1.0), (1, 1.0)):
+            nc.vector.tensor_scalar(
+                out=turns[:, :, 0:1, e],
+                in0=pos_i[:].unsqueeze(2),
+                scalar1=sign / (2.0 * math.pi),
+                scalar2=None,
+                op0=ALU.mult,
+            )
         for level in range(5):
             w = 1 << level
             nc.vector.tensor_scalar(
-                out=turns[:, :, w : 2 * w], in0=turns[:, :, 0:w], scalar1=RATIO**w, scalar2=None, op0=ALU.mult
+                out=turns[:, :, w : 2 * w, :], in0=turns[:, :, 0:w, :], scalar1=RATIO**w, scalar2=None, op0=ALU.mult
             )
-        whole = keep.tile([P, 2, T, NPAIRS], I32, name="whole")
-        nc.vector.tensor_scalar(out=whole[:, 0], in0=turns[:], scalar1=0.25, scalar2=None, op0=ALU.add)
+        whole = keep.tile([P, 2, T, NPAIRS, 2], I32, name="whole")
         nc.vector.tensor_copy(out=whole[:, 1], in_=turns[:])
-        frac = keep.tile([P, 2, T, NPAIRS], F32, name="frac")
-        nc.vector.tensor_tensor(out=frac[:, 0], in0=whole[:, 0], in1=turns[:], op=ALU.subtract)
+        nc.vector.tensor_scalar(out=whole[:, 0], in0=turns[:], scalar1=0.25, scalar2=None, op0=ALU.add)
+        frac = keep.tile([P, 2, T, NPAIRS, 2], F32, name="frac")
+        nc.vector.tensor_tensor(out=frac[:, 1], in0=turns[:], in1=whole[:, 1], op=ALU.subtract)
         nc.vector.scalar_tensor_tensor(
-            out=frac[:, 1], in0=whole[:, 1], scalar=0.25, in1=turns[:], op0=ALU.add, op1=ALU.subtract
+            out=frac[:, 0], in0=turns[:], scalar=0.25, in1=whole[:, 0], op0=ALU.add, op1=ALU.subtract
         )
-        half_sin = keep.tile([P, 2, T, NPAIRS], F32, name="half_sin")
-        nc.scalar.activation(out=half_sin[:], in_=frac[:], func=ACT.Sin, scale=math.pi)
-        half_sq = keep.tile([P, 2, T, NPAIRS], F32, name="half_sq")
-        nc.scalar.activation(out=half_sq[:], in_=half_sin[:], func=ACT.Square)
         cos_t = keep.tile([P, T, 2, 2 * NPAIRS], F32, name="cos_t")
         sin_t = keep.tile([P, T, NPAIRS, 2], F32, name="sin_t")
-
-        def tables():
-            for h in range(2):
-                nc.vector.tensor_scalar(
-                    out=cos_t[:, :, h, :].rearrange("p t (i e) -> p t i e", e=2),
-                    in0=half_sq[:, 0].unsqueeze(3).to_broadcast([P, T, NPAIRS, 2]),
-                    scalar1=-2.0,
-                    scalar2=1.0,
-                    op0=ALU.mult,
-                    op1=ALU.add,
-                )
-            for e, sign in ((0, -1.0), (1, 1.0)):
-                nc.vector.tensor_scalar(
-                    out=sin_t[:, :, :, e],
-                    in0=half_sq[:, 1],
-                    scalar1=-2.0 * sign,
-                    scalar2=sign,
-                    op0=ALU.mult,
-                    op1=ALU.add,
-                )
+        nc.scalar.activation(out=sin_t[:], in_=frac[:, 1], func=ACT.Sin, scale=2.0 * math.pi)
+        nc.scalar.activation(
+            out=cos_t[:],
+            in_=frac[:, 0].rearrange("p t i e -> p t (i e)").unsqueeze(2).to_broadcast([P, T, 2, 2 * NPAIRS]),
+            func=ACT.Sin,
+            scale=2.0 * math.pi,
+        )
 
         wgrp = keep.tile([P, 2, 2, 2, 2, 64, 4], BF16, name="wgrp", align_bytes=64)
         wcodes = keep.tile([P, 2, 512], U32, name="wcodes", align_bytes=64)
@@ -128,10 +114,7 @@ def tile_mla_pa_t_kernel(tc, x, Wq, Wk, out_0, out_1):
                 for qk in range(2):
                     src = wraw[:, qk, 4 * g : 4 * g + 4, :].rearrange("p t (h s c) -> p t h s c", h=2, s=2)
                     permuted = src[:, :, :, 1 - s, :].rearrange("p t h c -> p h c t")
-                    if (g, s, qk) in S_REGROUP:
-                        nc.scalar.copy(out=wgrp[:, g, s, qk], in_=permuted)
-                    else:
-                        nc.vector.tensor_copy(out=wgrp[:, g, s, qk], in_=permuted)
+                    nc.vector.tensor_copy(out=wgrp[:, g, s, qk], in_=permuted)
 
         def quantise_weights(g):
             nc.vector.quantize_mx(
@@ -172,51 +155,44 @@ def tile_mla_pa_t_kernel(tc, x, Wq, Wk, out_0, out_1):
                 )
             live[("grp", n)] = grp
 
-        def quantise(n, pieces):
+        def quantise(n):
             grp = live[("grp", n)][:].rearrange("p a g r t -> p (a g r t)")
             codes = work.tile([P, 512], U32, name="codes", align_bytes=64)
             scales = work.tile([P, 512], U8, name="scales", align_bytes=64)
-            width = 512 // pieces
-            for piece in range(pieces):
-                cols = slice(piece * width, (piece + 1) * width)
-                nc.vector.quantize_mx(
-                    out=codes[:, cols].bitcast(FP8X4),
-                    scales=scales[:, cols],
-                    in_=grp[:, 4 * piece * width : 4 * (piece + 1) * width],
-                )
+            nc.vector.quantize_mx(out=codes[:].bitcast(FP8X4), scales=scales[:], in_=grp)
             live[("q", n)] = (codes, scales)
 
-        def multiply(n):
+        def multiply(n, s):
             codes, scales = live[("q", n)]
-            rope = ps_r.tile([P, 512], F32, name="rope")
-            nope = ps_n.tile([P, 512], F32, name="nope")
-            for s, bank in ((ROPE, rope), (NOPE, nope)):
-                for a in range(2):
-                    for g in range(2):
-                        col = (2 * a + g) * P
-                        nc.tensor.matmul_mx(
-                            out=bank[:, 256 * a : 256 * a + 256],
-                            lhsT=codes[:, col : col + P].bitcast(FP8X4),
-                            lhsT_scale=scales[:, col : col + P],
-                            rhs=wcodes[:, g, 256 * s : 256 * s + 256].bitcast(FP8X4),
-                            rhs_scale=wscales[:, g, 256 * s : 256 * s + 256],
-                            start=(g == 0),
-                            stop=(g == 1),
-                        )
-            live[("rope", n)] = rope
-            live[("nope", n)] = nope
+            if s == ROPE:
+                bank = ps_r.tile([P, 512], F32, name="rope")
+            else:
+                bank = ps_n.tile([P, 512], F32, name="nope")
+            live[(s, n)] = bank
+            for a in range(2):
+                for g in range(2):
+                    col = (2 * a + g) * P
+                    nc.tensor.matmul_mx(
+                        out=bank[:, 256 * a : 256 * a + 256],
+                        lhsT=codes[:, col : col + P].bitcast(FP8X4),
+                        lhsT_scale=scales[:, col : col + P],
+                        rhs=wcodes[:, g, 256 * s : 256 * s + 256].bitcast(FP8X4),
+                        rhs_scale=wscales[:, g, 256 * s : 256 * s + 256],
+                        start=(g == 0),
+                        stop=(g == 1),
+                    )
 
         def plain_out(n):
             b, t0 = where(n)
             dst = out_of[n].rearrange("p q (a h s c) -> p q a h s c", a=2, h=2, s=2)
             nc.scalar.copy(
                 out=dst[:, :, :, :, 0, :],
-                in_=live[("nope", n)][:].rearrange("p (a q h c) -> p q a h c", a=2, q=2, h=2),
+                in_=live[(NOPE, n)][:].rearrange("p (a q h c) -> p q a h c", a=2, q=2, h=2),
             )
 
         def products(n):
             b, t0 = where(n)
-            rope = live[("rope", n)]
+            rope = live[(ROPE, n)]
             dst = out_of[n].rearrange("p q (a h s c) -> p q a h s c", a=2, h=2, s=2)
             nc.vector.tensor_tensor(
                 out=dst[:, :, :, :, 1, :],
@@ -252,26 +228,33 @@ def tile_mla_pa_t_kernel(tc, x, Wq, Wk, out_0, out_1):
                         in_=og[:, :, qk, :],
                     )
 
-        for n in range(AHEAD):
+        regroup_weights(0)
+        quantise_weights(0)
+        regroup_weights(1)
+        quantise_weights(1)
+        for n in range(3):
             transposes(n)
             regroup(n)
-            if n == 0:
-                regroup_weights(0)
-                regroup_weights(1)
-                quantise_weights(0)
-                quantise_weights(1)
-        for n in range(QUANT_AHEAD):
-            quantise(n, 1)
-            if n == 0:
-                tables()
-        for n in range(N_UNITS):
-            multiply(n)
-            if n + AHEAD < N_UNITS:
-                transposes(n + AHEAD)
-            products(n)
-            if n + QUANT_AHEAD < N_UNITS:
-                quantise(n + QUANT_AHEAD, 1)
-            plain_out(n)
-            if n + AHEAD < N_UNITS:
-                regroup(n + AHEAD)
-            add_and_store(n)
+        quantise(0)
+        quantise(1)
+        steps = [((0,), (2,), (3, 4))]
+        steps += [((n, n + 1), (n + 2, n + 3), (n + 4, n + 5)) for n in range(1, N_UNITS - 1, 2)]
+        steps += [((N_UNITS - 1,), (), ())]
+        for now, quantised, ahead in steps:
+            for s in (ROPE, NOPE):
+                for n in now:
+                    multiply(n, s)
+            for n in ahead:
+                if n < N_UNITS:
+                    transposes(n)
+            for i, n in enumerate(now):
+                products(n)
+                if i < len(quantised) and quantised[i] < N_UNITS:
+                    quantise(quantised[i])
+            for n in now:
+                plain_out(n)
+            for n in ahead:
+                if n < N_UNITS:
+                    regroup(n)
+            for n in now:
+                add_and_store(n)

@@ -24,7 +24,6 @@ NOPE = 1
 FLOPS = 2 * 4096 * 1024 * 512
 
 N_UNITS = 16
-GP_ADD_UNTIL = 15
 
 
 def tile_mla_pa_t_kernel(tc, x, Wq, Wk, out_0, out_1):
@@ -40,16 +39,14 @@ def tile_mla_pa_t_kernel(tc, x, Wq, Wk, out_0, out_1):
         x_view = x.rearrange("b (p t) k -> b p t k", t=T)
         out_views = [o.rearrange("b (p t) h d -> b p t (h d)", t=T) for o in (out_0, out_1)]
 
-        chunks = [(0, 0, 1), (0, 1, 1), (0, 2, 1), (0, 3, 1), (0, 4, 2), (0, 6, 2), (1, 0, 4), (1, 4, 4), (2, 0, 8), (3, 0, 8)]
         x_words = {}
-        wraw = keep.tile([P, 2, 8, 256], BF16, name="wraw")
+        wraw = keep.tile([P, 2, 2, 4, 256], BF16, name="wraw")
 
-        def load_w(g):
-            for qk, w_dram in enumerate((Wq, Wk)):
-                nc.sync.dma_start(
-                    out=wraw[:, qk, 4 * g : 4 * g + 4, :],
-                    in_=w_dram.rearrange("(g p t) c -> g p t c", g=2, t=4)[g],
-                )
+        def load_w(qk, g):
+            nc.sync.dma_start(
+                out=wraw[:, qk, g],
+                in_=(Wq, Wk)[qk].rearrange("(g p t) c -> g p t c", g=2, t=4)[g],
+            )
 
         def load_x(b, t0, nt):
             xs = keep.tile([P, nt, DIM], BF16, name="x%d_%d" % (b, t0))
@@ -57,12 +54,17 @@ def tile_mla_pa_t_kernel(tc, x, Wq, Wk, out_0, out_1):
             for t in range(nt):
                 x_words[(b, t0 + t)] = xs[:, t, :].bitcast(F32)
 
-        load_w(0)
-        load_x(*chunks[0])
-        load_x(*chunks[1])
-        load_w(1)
-        for chunk in chunks[2:]:
-            load_x(*chunk)
+        load_x(0, 0, 1)
+        load_x(0, 1, 1)
+        load_w(0, 0)
+        load_w(0, 1)
+        for t in range(2, 6):
+            load_x(0, t, 1)
+        load_w(1, 0)
+        load_w(1, 1)
+        load_x(0, 6, 2)
+        for b, t0, nt in ((1, 0, 4), (1, 4, 4), (2, 0, 8), (3, 0, 8)):
+            load_x(b, t0, nt)
 
         zero = keep.tile([P, 1], F32, name="zero")
         nc.vector.memset(zero[:], 0.0)
@@ -97,33 +99,36 @@ def tile_mla_pa_t_kernel(tc, x, Wq, Wk, out_0, out_1):
         )
         cos_t = keep.tile([P, T, 2, 2 * NPAIRS], F32, name="cos_t")
         sin_t = keep.tile([P, T, NPAIRS, 2], F32, name="sin_t")
-        nc.scalar.activation(out=sin_t[:], in_=frac[:, 1], func=ACT.Sin, scale=2.0 * math.pi)
-        nc.scalar.activation(
-            out=cos_t[:],
-            in_=frac[:, 0].rearrange("p t i e -> p t (i e)").unsqueeze(2).to_broadcast([P, T, 2, 2 * NPAIRS]),
-            func=ACT.Sin,
-            scale=2.0 * math.pi,
-        )
 
-        wgrp = keep.tile([P, 2, 2, 2, 2, 64, 4], BF16, name="wgrp", align_bytes=64)
-        wcodes = keep.tile([P, 2, 512], U32, name="wcodes", align_bytes=64)
-        wscales = keep.tile([P, 2, 512], U8, name="wscales", align_bytes=64)
+        def sines():
+            nc.scalar.activation(out=sin_t[:], in_=frac[:, 1], func=ACT.Sin, scale=2.0 * math.pi)
 
-        def regroup_weights(g):
-            for s in (ROPE, NOPE):
-                for qk in range(2):
-                    src = wraw[:, qk, 4 * g : 4 * g + 4, :].rearrange("p t (h s c) -> p t h s c", h=2, s=2)
-                    permuted = src[:, :, :, 1 - s, :].rearrange("p t h c -> p h c t")
-                    nc.vector.tensor_copy(out=wgrp[:, g, s, qk], in_=permuted)
-
-        def quantise_weights(g):
-            nc.vector.quantize_mx(
-                out=wcodes[:, g, :].bitcast(FP8X4),
-                scales=wscales[:, g, :],
-                in_=wgrp[:, g].rearrange("p s q h c t -> p (s q h c t)"),
+        def cosines():
+            nc.scalar.activation(
+                out=cos_t[:],
+                in_=frac[:, 0].rearrange("p t i e -> p t (i e)").unsqueeze(2).to_broadcast([P, T, 2, 2 * NPAIRS]),
+                func=ACT.Sin,
+                scale=2.0 * math.pi,
             )
 
-        groups = [(n, n + 1) for n in range(0, N_UNITS - 2, 2)] + [(N_UNITS - 2,), (N_UNITS - 1,)]
+        wgrp = keep.tile([P, 2, 2, 2, 2, 64, 4], BF16, name="wgrp", align_bytes=64)
+        wcodes = keep.tile([P, 2, 2, 2, P], U32, name="wcodes", align_bytes=64)
+        wscales = keep.tile([P, 2, 2, 2, P], U8, name="wscales", align_bytes=64)
+
+        def weights(qk):
+            for g in range(2):
+                for s in (ROPE, NOPE):
+                    src = wraw[:, qk, g].rearrange("p t (h s c) -> p h s c t", h=2, s=2)
+                    nc.vector.tensor_copy(out=wgrp[:, qk, g, s], in_=src[:, :, 1 - s])
+            for g in range(2):
+                for s in (ROPE, NOPE):
+                    nc.vector.quantize_mx(
+                        out=wcodes[:, g, s, qk].bitcast(FP8X4),
+                        scales=wscales[:, g, s, qk],
+                        in_=wgrp[:, qk, g, s].rearrange("p h c t -> p (h c t)"),
+                    )
+
+        groups = [(n, n + 1) for n in range(0, 10, 2)] + [(n,) for n in range(10, N_UNITS)]
         out_of = {}
         last_of = {}
         for group in groups:
@@ -162,22 +167,23 @@ def tile_mla_pa_t_kernel(tc, x, Wq, Wk, out_0, out_1):
             nc.vector.quantize_mx(out=codes[:].bitcast(FP8X4), scales=scales[:], in_=grp)
             live[("q", n)] = (codes, scales)
 
-        def multiply(n, s):
+        def multiply(n, s, qs):
             codes, scales = live[("q", n)]
-            if s == ROPE:
-                bank = ps_r.tile([P, 512], F32, name="rope")
-            else:
-                bank = ps_n.tile([P, 512], F32, name="nope")
-            live[(s, n)] = bank
+            if (s, n) not in live:
+                if s == ROPE:
+                    live[(s, n)] = ps_r.tile([P, 2, 2, P], F32, name="rope")
+                else:
+                    live[(s, n)] = ps_n.tile([P, 2, 2, P], F32, name="nope")
+            bank = live[(s, n)]
             for a in range(2):
                 for g in range(2):
                     col = (2 * a + g) * P
                     nc.tensor.matmul_mx(
-                        out=bank[:, 256 * a : 256 * a + 256],
+                        out=bank[:, a, qs].rearrange("p q c -> p (q c)"),
                         lhsT=codes[:, col : col + P].bitcast(FP8X4),
                         lhsT_scale=scales[:, col : col + P],
-                        rhs=wcodes[:, g, 256 * s : 256 * s + 256].bitcast(FP8X4),
-                        rhs_scale=wscales[:, g, 256 * s : 256 * s + 256],
+                        rhs=wcodes[:, g, s, qs].rearrange("p q c -> p (q c)").bitcast(FP8X4),
+                        rhs_scale=wscales[:, g, s, qs].rearrange("p q c -> p (q c)"),
                         start=(g == 0),
                         stop=(g == 1),
                     )
@@ -187,74 +193,93 @@ def tile_mla_pa_t_kernel(tc, x, Wq, Wk, out_0, out_1):
             dst = out_of[n].rearrange("p q (a h s c) -> p q a h s c", a=2, h=2, s=2)
             nc.scalar.copy(
                 out=dst[:, :, :, :, 0, :],
-                in_=live[(NOPE, n)][:].rearrange("p (a q h c) -> p q a h c", a=2, q=2, h=2),
+                in_=live[(NOPE, n)][:].rearrange("p a q (h c) -> p q a h c", h=2),
             )
 
-        def products(n):
+        def products(n, qs):
             b, t0 = where(n)
+            nq = qs.stop - qs.start
             rope = live[(ROPE, n)]
             dst = out_of[n].rearrange("p q (a h s c) -> p q a h s c", a=2, h=2, s=2)
             nc.vector.tensor_tensor(
-                out=dst[:, :, :, :, 1, :],
-                in0=rope[:].rearrange("p (a q h c) -> p q a h c", a=2, q=2, h=2),
-                in1=cos_t[:, t0 : t0 + 2].unsqueeze(1).to_broadcast([P, 2, 2, 2, 2 * NPAIRS]),
+                out=dst[:, qs, :, :, 1, :],
+                in0=rope[:].rearrange("p a q (h c) -> p q a h c", h=2)[:, qs],
+                in1=cos_t[:, t0 : t0 + 2].unsqueeze(1).to_broadcast([P, nq, 2, 2, 2 * NPAIRS]),
                 op=ALU.mult,
             )
-            cross = work.tile([P, 2, 4, NPAIRS, 2], F32, name="cross")
+            cross = work.tile([P, 2, nq, 2, NPAIRS, 2], F32, name="cross")
             nc.vector.tensor_tensor(
-                out=cross[:],
-                in0=rope[:].rearrange("p (a qh i e) -> p a qh i e", a=2, qh=4, e=2)[:, :, :, :, ::-1],
-                in1=sin_t[:, t0 : t0 + 2].unsqueeze(2).to_broadcast([P, 2, 4, NPAIRS, 2]),
+                out=cross[:].rearrange("p a q h i e -> p a (q h) i e"),
+                in0=rope[:].rearrange("p a q (h i e) -> p a q h i e", h=2, e=2)[:, :, qs, :, :, ::-1].rearrange(
+                    "p a q h i e -> p a (q h) i e"
+                ),
+                in1=sin_t[:, t0 : t0 + 2].unsqueeze(2).to_broadcast([P, 2, 2 * nq, NPAIRS, 2]),
                 op=ALU.mult,
             )
-            live[("cross", n)] = cross
+            live[("cross", n, qs.start)] = cross
 
-        def add_and_store(n):
-            b, t0 = where(n)
-            eng = nc.gpsimd if n < GP_ADD_UNTIL else nc.vector
-            rot = out_of[n].rearrange("p q (a h s c) -> p q a h s c", a=2, h=2, s=2)
-            eng.tensor_tensor(
-                out=rot[:, :, :, :, 1, :],
-                in0=rot[:, :, :, :, 1, :],
-                in1=live[("cross", n)][:].rearrange("p a (q h) i e -> p q a h (i e)", h=2),
-                op=ALU.add,
+        def add(n, engine, qs):
+            rot = out_of[n].rearrange("p q (a h s c) -> p q a h s c", a=2, h=2, s=2)[:, qs, :, :, 1, :]
+            cross = live[("cross", n, qs.start)]
+            engine.tensor_tensor(
+                out=rot, in0=rot, in1=cross[:].rearrange("p a q h i e -> p q a h (i e)"), op=ALU.add
             )
-            if n in last_of:
-                og, group = last_of[n]
-                gb, gt0 = where(group[0])
-                for qk in range(2):
-                    nc.sync.dma_start(
-                        out=out_views[qk][gb][:, gt0 : gt0 + 2 * len(group), :].rearrange("p (u a) d -> p u (a d)", a=2),
-                        in_=og[:, :, qk, :],
-                    )
 
-        regroup_weights(0)
-        quantise_weights(0)
-        regroup_weights(1)
-        quantise_weights(1)
-        for n in range(3):
-            transposes(n)
-            regroup(n)
-        quantise(0)
-        quantise(1)
-        steps = [((0,), (2,), (3, 4))]
-        steps += [((n, n + 1), (n + 2, n + 3), (n + 4, n + 5)) for n in range(1, N_UNITS - 1, 2)]
-        steps += [((N_UNITS - 1,), (), ())]
-        for now, quantised, ahead in steps:
+        def store(n):
+            og, group = last_of[n]
+            b, t0 = where(group[0])
+            for qk in range(2):
+                nc.sync.dma_start(
+                    out=out_views[qk][b][:, t0 : t0 + 2 * len(group), :].rearrange("p (u a) d -> p u (a d)", a=2),
+                    in_=og[:, :, qk, :],
+                )
+
+        both = slice(0, 2)
+        only = (slice(0, 1), slice(1, 2))
+
+        transposes(0)
+        regroup(0)
+        sines()
+        weights(0)
+        transposes(1)
+        regroup(1)
+        cosines()
+        transposes(2)
+        regroup(2)
+        for n in range(2):
+            quantise(n)
             for s in (ROPE, NOPE):
-                for n in now:
-                    multiply(n, s)
-            for n in ahead:
-                if n < N_UNITS:
-                    transposes(n)
-            for i, n in enumerate(now):
-                products(n)
-                if i < len(quantised) and quantised[i] < N_UNITS:
-                    quantise(quantised[i])
-            for n in now:
-                plain_out(n)
-            for n in ahead:
-                if n < N_UNITS:
-                    regroup(n)
-            for n in now:
-                add_and_store(n)
+                multiply(n, s, only[0])
+        weights(1)
+        quantise(2)
+        transposes(3)
+        regroup(3)
+        last = N_UNITS - 1
+        for n in range(N_UNITS):
+            for s in (ROPE, NOPE):
+                multiply(n, s, only[1] if n < 2 else both)
+            if n + 4 < N_UNITS:
+                transposes(n + 4)
+            if n < last - 1:
+                products(n, both)
+            else:
+                products(n, only[0])
+                if n == last:
+                    add(n - 1, nc.vector, only[0])
+                products(n, only[1])
+            if n + 3 < N_UNITS:
+                quantise(n + 3)
+            plain_out(n)
+            if n + 4 < N_UNITS:
+                regroup(n + 4)
+            if n < last - 1:
+                add(n, nc.gpsimd, both)
+                if n in last_of:
+                    store(n)
+            elif n == last - 1:
+                add(n, nc.gpsimd, only[1])
+            else:
+                store(n - 1)
+                for qs in only:
+                    add(n, nc.vector, qs)
+                store(n)

@@ -141,14 +141,22 @@ def tile_mla_pa_t_kernel(tc, x, Wq, Wk, out_0, out_1):
         def where(n):
             return n // 4, 2 * (n % 4)
 
+        def reorder(n, a, copy):
+            b, t0 = where(n)
+            ordered = work.tile([P, 2, 2, P], F32, name="ordered")
+            copy(out=ordered[:], in_=x_words[(b, t0 + a)].rearrange("r (g p u) -> r g u p", g=2, u=2))
+            live[("ordered", n, a)] = ordered
+
         def transposes(n):
             b, t0 = where(n)
             for a in range(2):
                 xt = ps_t.tile([P, 4, P], F32, name="xt")
                 for j in range(4):
-                    nc.tensor.transpose(
-                        out=xt[:, j, :], in_=x_words[(b, t0 + a)][:, 256 * (j // 2) + j % 2 : 256 * (j // 2 + 1) : 2], identity=ident[:]
-                    )
+                    if ("ordered", n, a) in live:
+                        words = live[("ordered", n, a)][:, j // 2, j % 2]
+                    else:
+                        words = x_words[(b, t0 + a)][:, 256 * (j // 2) + j % 2 : 256 * (j // 2 + 1) : 2]
+                    nc.tensor.transpose(out=xt[:, j, :], in_=words, identity=ident[:])
                 live[("xt", n, a)] = xt
 
         def regroup(n):
@@ -269,6 +277,8 @@ def tile_mla_pa_t_kernel(tc, x, Wq, Wk, out_0, out_1):
                 products(n, only[1])
             if n + 3 < N_UNITS:
                 quantise(n + 3)
+            if n % 2 == 0 and n + 5 < N_UNITS:
+                reorder(n + 5, 0, nc.scalar.copy)
             plain_out(n)
             if n + 4 < N_UNITS:
                 regroup(n + 4)

import math
from contextlib import ExitStack

import concourse.mybir as mybir
from concourse.masks import make_identity

F32 = mybir.dt.float32
BF16 = mybir.dt.bfloat16
I32 = mybir.dt.int32
U32 = mybir.dt.uint32
U8 = mybir.dt.uint8
FP8X4 = mybir.dt.float8_e4m3fn_x4
ALU = mybir.AluOpType
ACT = mybir.ActivationFunctionType

P = 128
B = 4
T = 8
DIM = 1024
NPAIRS = 32
RATIO = 10000.0 ** (-1.0 / 32.0)
ROPE = 0
NOPE = 1
FLOPS = 2 * 4096 * 1024 * 512

N_UNITS = 16


def tile_mla_pa_t_kernel(tc, x, Wq, Wk, out_0, out_1):
    nc = tc.nc
    with ExitStack() as ctx:
        ctx.enter_context(tc.manual_schedule())
        keep = ctx.enter_context(tc.tile_pool(name="keep", bufs=1))
        work = ctx.enter_context(tc.tile_pool(name="work", bufs=6))
        ps_t = ctx.enter_context(tc.psum_pool(name="ps_t", bufs=4))
        ps_r = ctx.enter_context(tc.psum_pool(name="ps_r", bufs=2))
        ps_n = ctx.enter_context(tc.psum_pool(name="ps_n", bufs=2))

        x_view = x.rearrange("b (p t) k -> b p t k", t=T)
        out_views = [o.rearrange("b (p t) h d -> b p t (h d)", t=T) for o in (out_0, out_1)]

        x_words = {}
        wraw = keep.tile([P, 2, 2, 4, 256], BF16, name="wraw")

        def load_w(qk, g):
            nc.sync.dma_start(
                out=wraw[:, qk, g],
                in_=(Wq, Wk)[qk].rearrange("(g p t) c -> g p t c", g=2, t=4)[g],
            )

        def load_x(b, t0, nt):
            xs = keep.tile([P, nt, DIM], BF16, name="x%d_%d" % (b, t0))
            nc.sync.dma_start(out=xs[:], in_=x_view[b][:, t0 : t0 + nt, :])
            for t in range(nt):
                x_words[(b, t0 + t)] = xs[:, t, :].bitcast(F32)

        load_x(0, 0, 1)
        load_x(0, 1, 1)
        load_w(0, 0)
        load_w(0, 1)
        for t in range(2, 6):
            load_x(0, t, 1)
        load_w(1, 0)
        load_w(1, 1)
        load_x(0, 6, 2)
        for b, t0, nt in ((1, 0, 4), (1, 4, 4), (2, 0, 8), (3, 0, 8)):
            load_x(b, t0, nt)

        zero = keep.tile([P, 1], F32, name="zero")
        nc.vector.memset(zero[:], 0.0)
        warm = keep.tile([P, 1], F32, name="warm")
        nc.scalar.activation(out=warm[:], in_=zero[:], func=ACT.Sin)
        pos_i = keep.tile([P, T], I32, name="pos_i")
        nc.gpsimd.iota(pos_i[:], pattern=[[1, T]], base=0, channel_multiplier=T)
        ident = keep.tile([P, P], F32, name="ident")
        make_identity(nc, ident[:])

        turns = keep.tile([P, T, NPAIRS, 2], F32, name="turns")
        for e, sign in ((0, -1.0), (1, 1.0)):
            nc.vector.tensor_scalar(
                out=turns[:, :, 0:1, e],
                in0=pos_i[:].unsqueeze(2),
                scalar1=sign / (2.0 * math.pi),
                scalar2=None,
                op0=ALU.mult,
            )
        for level in range(5):
            w = 1 << level
            nc.vector.tensor_scalar(
                out=turns[:, :, w : 2 * w, :], in0=turns[:, :, 0:w, :], scalar1=RATIO**w, scalar2=None, op0=ALU.mult
            )
        whole = keep.tile([P, 2, T, NPAIRS, 2], I32, name="whole")
        nc.vector.tensor_copy(out=whole[:, 1], in_=turns[:])
        nc.vector.tensor_scalar(out=whole[:, 0], in0=turns[:], scalar1=0.25, scalar2=None, op0=ALU.add)
        frac = keep.tile([P, 2, T, NPAIRS, 2], F32, name="frac")
        nc.vector.tensor_tensor(out=frac[:, 1], in0=turns[:], in1=whole[:, 1], op=ALU.subtract)
        nc.vector.scalar_tensor_tensor(
            out=frac[:, 0], in0=turns[:], scalar=0.25, in1=whole[:, 0], op0=ALU.add, op1=ALU.subtract
        )
        cos_t = keep.tile([P, T, 2, 2 * NPAIRS], F32, name="cos_t")
        sin_t = keep.tile([P, T, NPAIRS, 2], F32, name="sin_t")

        def sines():
            nc.scalar.activation(out=sin_t[:], in_=frac[:, 1], func=ACT.Sin, scale=2.0 * math.pi)

        def cosines():
            nc.scalar.activation(
                out=cos_t[:],
                in_=frac[:, 0].rearrange("p t i e -> p t (i e)").unsqueeze(2).to_broadcast([P, T, 2, 2 * NPAIRS]),
                func=ACT.Sin,
                scale=2.0 * math.pi,
            )

        wgrp = keep.tile([P, 2, 2, 2, 2, 64, 4], BF16, name="wgrp", align_bytes=64)
        wcodes = keep.tile([P, 2, 2, 2, P], U32, name="wcodes", align_bytes=64)
        wscales = keep.tile([P, 2, 2, 2, P], U8, name="wscales", align_bytes=64)

        def weights(qk):
            for g in range(2):
                for s in (ROPE, NOPE):
                    src = wraw[:, qk, g].rearrange("p t (h s c) -> p h s c t", h=2, s=2)
                    nc.vector.tensor_copy(out=wgrp[:, qk, g, s], in_=src[:, :, 1 - s])
            for g in range(2):
                for s in (ROPE, NOPE):
                    nc.vector.quantize_mx(
                        out=wcodes[:, g, s, qk].bitcast(FP8X4),
                        scales=wscales[:, g, s, qk],
                        in_=wgrp[:, qk, g, s].rearrange("p h c t -> p (h c t)"),
                    )

        groups = [(n, n + 1) for n in range(0, 10, 2)] + [(n,) for n in range(10, N_UNITS)]
        out_of = {}
        last_of = {}
        for group in groups:
            og = keep.tile([P, len(group), 2, 512], F32, name="og%d" % group[0])
            for u, n in enumerate(group):
                out_of[n] = og[:, u]
            last_of[group[-1]] = (og, group)
        live = {}

        def where(n):
            return n // 4, 2 * (n % 4)

        def reorder(n, a, copy):
            b, t0 = where(n)
            ordered = work.tile([P, 2, 2, P], F32, name="ordered")
            copy(out=ordered[:], in_=x_words[(b, t0 + a)].rearrange("r (g p u) -> r g u p", g=2, u=2))
            live[("ordered", n, a)] = ordered

        def transposes(n):
            b, t0 = where(n)
            for a in range(2):
                xt = ps_t.tile([P, 4, P], F32, name="xt")
                for j in range(4):
                    if ("ordered", n, a) in live:
                        words = live[("ordered", n, a)][:, j // 2, j % 2]
                    else:
                        words = x_words[(b, t0 + a)][:, 256 * (j // 2) + j % 2 : 256 * (j // 2 + 1) : 2]
                    nc.tensor.transpose(out=xt[:, j, :], in_=words, identity=ident[:])
                live[("xt", n, a)] = xt

        def regroup(n):
            grp = work.tile([P, 2, 2, P, 4], BF16, name="grp", align_bytes=64)
            grp_words = grp[:].bitcast(F32)
            for a in range(2):
                nc.scalar.copy(
                    out=grp_words[:, a], in_=live[("xt", n, a)][:].rearrange("p (g u) r -> p g r u", u=2)
                )
            live[("grp", n)] = grp

        def quantise(n):
            grp = live[("grp", n)][:].rearrange("p a g r t -> p (a g r t)")
            codes = work.tile([P, 512], U32, name="codes", align_bytes=64)
            scales = work.tile([P, 512], U8, name="scales", align_bytes=64)
            nc.vector.quantize_mx(out=codes[:].bitcast(FP8X4), scales=scales[:], in_=grp)
            live[("q", n)] = (codes, scales)

        def multiply(n, s, qs):
            codes, scales = live[("q", n)]
            if (s, n) not in live:
                if s == ROPE:
                    live[(s, n)] = ps_r.tile([P, 2, 2, P], F32, name="rope")
                else:
                    live[(s, n)] = ps_n.tile([P, 2, 2, P], F32, name="nope")
            bank = live[(s, n)]
            for a in range(2):
                for g in range(2):
                    col = (2 * a + g) * P
                    nc.tensor.matmul_mx(
                        out=bank[:, a, qs].rearrange("p q c -> p (q c)"),
                        lhsT=codes[:, col : col + P].bitcast(FP8X4),
                        lhsT_scale=scales[:, col : col + P],
                        rhs=wcodes[:, g, s, qs].rearrange("p q c -> p (q c)").bitcast(FP8X4),
                        rhs_scale=wscales[:, g, s, qs].rearrange("p q c -> p (q c)"),
                        start=(g == 0),
                        stop=(g == 1),
                    )

        def plain_out(n):
            b, t0 = where(n)
            dst = out_of[n].rearrange("p q (a h s c) -> p q a h s c", a=2, h=2, s=2)
            nc.scalar.copy(
                out=dst[:, :, :, :, 0, :],
                in_=live[(NOPE, n)][:].rearrange("p a q (h c) -> p q a h c", h=2),
            )

        def products(n, qs):
            b, t0 = where(n)
            nq = qs.stop - qs.start
            rope = live[(ROPE, n)]
            dst = out_of[n].rearrange("p q (a h s c) -> p q a h s c", a=2, h=2, s=2)
            nc.vector.tensor_tensor(
                out=dst[:, qs, :, :, 1, :],
                in0=rope[:].rearrange("p a q (h c) -> p q a h c", h=2)[:, qs],
                in1=cos_t[:, t0 : t0 + 2].unsqueeze(1).to_broadcast([P, nq, 2, 2, 2 * NPAIRS]),
                op=ALU.mult,
            )
            cross = work.tile([P, 2, nq, 2, NPAIRS, 2], F32, name="cross")
            nc.vector.tensor_tensor(
                out=cross[:].rearrange("p a q h i e -> p a (q h) i e"),
                in0=rope[:].rearrange("p a q (h i e) -> p a q h i e", h=2, e=2)[:, :, qs, :, :, ::-1].rearrange(
                    "p a q h i e -> p a (q h) i e"
                ),
                in1=sin_t[:, t0 : t0 + 2].unsqueeze(2).to_broadcast([P, 2, 2 * nq, NPAIRS, 2]),
                op=ALU.mult,
            )
            live[("cross", n, qs.start)] = cross

        def add(n, engine, qs):
            rot = out_of[n].rearrange("p q (a h s c) -> p q a h s c", a=2, h=2, s=2)[:, qs, :, :, 1, :]
            cross = live[("cross", n, qs.start)]
            engine.tensor_tensor(
                out=rot, in0=rot, in1=cross[:].rearrange("p a q h i e -> p q a h (i e)"), op=ALU.add
            )

        def store(n):
            og, group = last_of[n]
            b, t0 = where(group[0])
            for qk in range(2):
                nc.sync.dma_start(
                    out=out_views[qk][b][:, t0 : t0 + 2 * len(group), :].rearrange("p (u a) d -> p u (a d)", a=2),
                    in_=og[:, :, qk, :],
                )

        both = slice(0, 2)
        only = (slice(0, 1), slice(1, 2))

        transposes(0)
        regroup(0)
        sines()
        weights(0)
        transposes(1)
        regroup(1)
        cosines()
        transposes(2)
        regroup(2)
        for n in range(2):
            quantise(n)
            for s in (ROPE, NOPE):
                multiply(n, s, only[0])
        weights(1)
        quantise(2)
        transposes(3)
        regroup(3)
        last = N_UNITS - 1
        for n in range(N_UNITS):
            for s in (ROPE, NOPE):
                multiply(n, s, only[1] if n < 2 else both)
            if n + 4 < N_UNITS:
                transposes(n + 4)
            if n < last - 1:
                products(n, both)
            else:
                products(n, only[0])
                if n == last:
                    add(n - 1, nc.vector, only[0])
                products(n, only[1])
            if n + 3 < N_UNITS:
                quantise(n + 3)
            if n % 2 == 0 and n + 5 < N_UNITS:
                reorder(n + 5, 0, nc.scalar.copy)
            plain_out(n)
            if n + 4 < N_UNITS:
                regroup(n + 4)
            if n < last - 1:
                add(n, nc.gpsimd, both)
                if n in last_of:
                    store(n)
            elif n == last - 1:
                add(n, nc.gpsimd, only[1])
            else:
                store(n - 1)
                for qs in only:
                    add(n, nc.vector, qs)
                store(n)
